import numpy as np
import ml_dtypes

BF16 = ml_dtypes.bfloat16


def bf(x):
    return np.asarray(x, np.float32).astype(BF16)


def f32(x):
    return np.asarray(x, np.float32)


def f64(x):
    return np.asarray(x).astype(np.float64)


def striped(idx):
    return np.tile(idx.reshape(-1, 16).T, (8, 1))


B, S, D, M, U, H, K, N = 2, 768, 128, 256, 4096, 384, 8, 3072
EPS = 1e-5


def setup_inputs():
    return {
        "table": bf(np.random.standard_normal((B, S, D))),
        "w_left": bf(np.random.standard_normal((D, M)) / np.sqrt(2.0 * D)),
        "w_right": bf(np.random.standard_normal((D, M)) / np.sqrt(2.0 * D)),
        "w_comb": f32(np.random.standard_normal((D + M, U)) / np.sqrt(D + M)),
        "b_comb": f32(0.2 * np.random.standard_normal((U, 1))),
        "w_ff": f32(np.random.standard_normal((U, D)) * np.sqrt(2.0 / U)),
        "norm_w": f32(1.0 + 0.1 * np.random.standard_normal((D, 1))),
        "norm_b": f32(0.1 * np.random.standard_normal((D, 1))),
        "offs": striped(np.concatenate([np.random.permutation(S)[:H] for _ in range(K)])),
    }


def reference(table, w_left, w_right, w_comb, b_comb, w_ff, norm_w, norm_b, offs):
    idx = offs[:16].T.reshape(-1)
    lst = idx.reshape(B, -1, S)
    t = f64(table)
    wl, wr, wc, wf = f64(w_left), f64(w_right), f64(w_comb), f64(w_ff)
    outs = []
    for b in range(B):
        cust = t[b].T
        info = wl.T @ t[b][lst[b, 0]].T + wr.T @ t[b][lst[b, 1]].T
        hid = np.maximum(wc[:D].T @ cust + wc[D:].T @ info + f64(b_comb), 0.0)
        added = cust + wf.T @ hid
        mean = added.mean(axis=1, keepdims=True)
        var = np.square(added - mean).mean(axis=1, keepdims=True)
        outs.append((added - mean) / np.sqrt(var + EPS) * f64(norm_w) + f64(norm_b))
    return np.concatenate(outs, axis=1)

@@ -1,0 +1,169 @@
+import concourse.masks as masks
+import concourse.mybir as mybir
+
+BF16, F32, U16 = mybir.dt.bfloat16, mybir.dt.float32, mybir.dt.uint16
+ACT = mybir.ActivationFunctionType
+ALU = mybir.AluOpType
+
+P = 128
+B, S = 2, 768
+M, U = 256, 4096
+EPS = 1e-5
+HALF = S // 2
+M_BLOCKS = M // P
+K_BLOCKS = 1 + M_BLOCKS
+U_BLOCKS = U // P
+CHUNK = 4
+CHUNKS = U_BLOCKS // CHUNK
+VECTOR_ROWS = 64
+GAIN, BIAS = U_BLOCKS, U_BLOCKS + 1
+
+FLOPS = 2 * B * S * (2 * P * M + (P + M) * U + U * P)
+
+
+def tile_messagepassinglayer_b_kernel(
+    tc, table, w_left, w_right, w_comb, b_comb, w_ff, norm_w, norm_b, offs, out
+):
+    nc = tc.nc
+    with (
+        tc.tile_pool(name="held", bufs=1) as held,
+        tc.tile_pool(name="ring", bufs=3) as ring,
+        tc.psum_pool(name="sums", bufs=1) as sums,
+        tc.psum_pool(name="work", bufs=4) as work,
+    ):
+        rows = [held.tile([P, S // P, P], BF16, name=f"rows{b}") for b in range(B)]
+        offsets = held.tile([P, B * 2 * S // 16], U16, name="offsets")
+        left = held.tile([P, M], BF16, name="left")
+        right = held.tile([P, M], BF16, name="right")
+        vectors = held.tile([VECTOR_ROWS, P], F32, name="vectors")
+        by_customer = table.rearrange("b (a p) d -> b p a d", p=P)
+        nc.vector.memset(vectors[:], 0.0)
+        nc.sync.dma_start(rows[0][:], by_customer[0])
+        nc.scalar.dma_start(rows[1][:], by_customer[1])
+        nc.sync.dma_start(offsets[:], offs)
+        nc.sync.dma_start(left[:], w_left)
+        nc.scalar.dma_start(right[:], w_right)
+        nc.scalar.dma_start(vectors[0:U_BLOCKS, :], b_comb.rearrange("(j p) o -> j (p o)", p=P))
+        nc.scalar.dma_start(vectors[GAIN : GAIN + 1, :], norm_w.rearrange("p o -> o p"))
+        nc.scalar.dma_start(vectors[BIAS : BIAS + 1, :], norm_b.rearrange("p o -> o p"))
+        comb_f32, ff_f32 = [], []
+        for c in range(CHUNKS):
+            span = slice(c * CHUNK * P, (c + 1) * CHUNK * P)
+            comb_f32.append(held.tile([P, K_BLOCKS, CHUNK * P], F32, name=f"comb_f32_{c}"))
+            nc.sync.dma_start(comb_f32[c][:], w_comb[:, span].rearrange("(k p) u -> p k u", p=P))
+            ff_f32.append(held.tile([P, CHUNK, P], F32, name=f"ff_f32_{c}"))
+            nc.sync.dma_start(ff_f32[c][:], w_ff[span, :].rearrange("(j p) c -> p j c", p=P))
+
+        identity = held.tile([P, P], BF16, name="identity")
+        masks.make_identity(nc, identity[:])
+        identity_f32 = held.tile([VECTOR_ROWS, VECTOR_ROWS], F32, name="identity_f32")
+        masks.make_identity(nc, identity_f32[:])
+        eps = held.tile([P, 1], F32, name="eps")
+        nc.vector.memset(eps[:], EPS)
+
+        window = [held.tile([P, S], BF16, name=f"window{b}") for b in range(B)]
+        for b in range(B):
+            turned = work.tile([P, S], BF16, tag="work", name="turned")
+            for a in range(S // P):
+                nc.tensor.transpose(turned[:, a * P : (a + 1) * P], rows[b][:, a, :], identity[:])
+            if b == 0:
+                nc.vector.tensor_copy(window[b][:], turned[:])
+            else:
+                nc.scalar.copy(window[b][:], turned[:])
+
+        columns_psum = work.tile([P, VECTOR_ROWS], F32, tag="work", name="columns_psum")
+        nc.tensor.transpose(columns_psum[:], vectors[:], identity_f32[:])
+        columns = held.tile([P, VECTOR_ROWS], F32, name="columns")
+        nc.vector.tensor_copy(columns[:], columns_psum[:])
+
+        comb, ff = {}, {}
+
+        def round_chunk(c):
+            comb[c] = held.tile([P, K_BLOCKS, CHUNK * P], BF16, name=f"comb{c}")
+            nc.vector.tensor_copy(comb[c][:], comb_f32[c][:])
+            ff[c] = held.tile([P, CHUNK, P], BF16, name=f"ff{c}")
+            nc.scalar.copy(ff[c][:], ff_f32[c][:])
+
+        round_chunk(0)
+
+        info = [[held.tile([P, S], BF16, name=f"info{b}_{m}") for m in range(M_BLOCKS)] for b in range(B)]
+        for b in range(B):
+            for h in range(2):
+                for m in range(M_BLOCKS):
+                    both = work.tile([P, HALF], F32, tag="work", name="both")
+                    for side, weights in enumerate((left, right)):
+                        first = ((2 * b + side) * S + h * HALF) // 16
+                        nc.tensor.matmul(
+                            both[:],
+                            weights[:, m * P : (m + 1) * P],
+                            window[b][:].indirect(offsets[:, first : first + HALF // 16]),
+                            start=side == 0,
+                            stop=side == 1,
+                        )
+                    rounded = info[b][m][:, h * HALF : (h + 1) * HALF]
+                    if m == 0:
+                        nc.scalar.copy(rounded, both[:])
+                    else:
+                        nc.vector.tensor_copy(rounded, both[:])
+
+        added = [[sums.tile([P, HALF], F32, name=f"added{b}_{h}") for h in range(2)] for b in range(B)]
+
+        def hidden_block(b, u):
+            c, j = divmod(u, CHUNK)
+            moving = (window[b], info[b][0], info[b][1])
+            pre = [work.tile([P, HALF], F32, tag="work", name=f"pre{h}") for h in range(2)]
+            for k in range(K_BLOCKS):
+                for h in range(2):
+                    nc.tensor.matmul(
+                        pre[h][:],
+                        comb[c][:, k, j * P : (j + 1) * P],
+                        moving[k][:, h * HALF : (h + 1) * HALF],
+                        start=k == 0,
+                        stop=k == K_BLOCKS - 1,
+                    )
+            hid = [ring.tile([P, HALF], BF16, name=f"hid{h}") for h in range(2)]
+            nc.scalar.activation(hid[0][:], pre[0][:], ACT.Relu, bias=columns[:, u : u + 1])
+            nc.vector.tensor_scalar(hid[1][:], pre[1][:], columns[:, u : u + 1], 0.0, op0=ALU.add, op1=ALU.max)
+            return hid
+
+        def feed_forward(b, u, hid):
+            c, j = divmod(u, CHUNK)
+            for h in range(2):
+                nc.tensor.matmul(added[b][h][:], ff[c][:, j, :], hid[h][:], start=False, stop=u == U_BLOCKS - 1)
+            if u == U_BLOCKS - 1:
+                normalise(b)
+
+        def normalise(b):
+            stats = ring.tile([P, 2 * 6], F32, name="stats")
+            for h in range(2):
+                nc.vector.bn_stats(stats[:, 6 * h : 6 * h + 6], added[b][h][:])
+            mean_var = ring.tile([P, 2], F32, name="mean_var")
+            nc.vector.bn_aggr(mean_var[:], stats[:])
+            std = ring.tile([P, 1], F32, name="std")
+            nc.scalar.activation(std[:], mean_var[:, 1:2], ACT.Sqrt, bias=eps[:])
+            gain = ring.tile([P, 1], F32, name="gain")
+            nc.vector.reciprocal(gain[:], std[:])
+            nc.vector.tensor_mul(gain[:], gain[:], columns[:, GAIN : GAIN + 1])
+            shift = ring.tile([P, 1], F32, name="shift")
+            nc.vector.tensor_mul(shift[:], mean_var[:, 0:1], gain[:])
+            nc.vector.tensor_sub(shift[:], columns[:, BIAS : BIAS + 1], shift[:])
+            normed = [ring.tile([P, HALF], F32, name=f"normed{h}") for h in range(2)]
+            nc.scalar.activation(normed[0][:], added[b][0][:], ACT.Identity, bias=shift[:], scale=gain[:])
+            nc.vector.tensor_scalar(normed[1][:], added[b][1][:], gain[:], shift[:], op0=ALU.mult, op1=ALU.add)
+            nc.scalar.dma_start(out[:, b * S : b * S + HALF], normed[0][:])
+            nc.sync.dma_start(out[:, b * S + HALF : (b + 1) * S], normed[1][:])
+
+        waiting = None
+        for b in range(B):
+            for h in range(2):
+                nc.tensor.matmul(
+                    added[b][h][:], identity[:], window[b][:, h * HALF : (h + 1) * HALF], start=True, stop=False
+                )
+            for u in range(U_BLOCKS):
+                if b == 0 and u % CHUNK == 0 and u // CHUNK + 1 < CHUNKS:
+                    round_chunk(u // CHUNK + 1)
+                hid = hidden_block(b, u)
+                if waiting is not None:
+                    feed_forward(*waiting)
+                waiting = (b, u, hid)
+        feed_forward(*waiting)

@@ -9,12 +9,14 @@ P = 128
 B, S = 2, 768
 M, U = 256, 4096
 EPS = 1e-5
+ROWS = S // P
 HALF = S // 2
 M_BLOCKS = M // P
 K_BLOCKS = 1 + M_BLOCKS
 U_BLOCKS = U // P
 CHUNK = 4
 CHUNKS = U_BLOCKS // CHUNK
+AHEAD = 4
 VECTOR_ROWS = 64
 GAIN, BIAS = U_BLOCKS, U_BLOCKS + 1
 
@@ -31,21 +33,18 @@ def tile_messagepassinglayer_b_kernel(
         tc.psum_pool(name="sums", bufs=1) as sums,
         tc.psum_pool(name="work", bufs=4) as work,
     ):
-        rows = [held.tile([P, S // P, P], BF16, name=f"rows{b}") for b in range(B)]
+        rows = [held.tile([P, ROWS, P], BF16, name=f"rows{b}") for b in range(B)]
         offsets = held.tile([P, B * 2 * S // 16], U16, name="offsets")
         left = held.tile([P, M], BF16, name="left")
         right = held.tile([P, M], BF16, name="right")
         vectors = held.tile([VECTOR_ROWS, P], F32, name="vectors")
-        by_customer = table.rearrange("b (a p) d -> b p a d", p=P)
+        by_customer = table.rearrange("b (p a) d -> b p a d", a=ROWS)
         nc.vector.memset(vectors[:], 0.0)
         nc.sync.dma_start(rows[0][:], by_customer[0])
-        nc.scalar.dma_start(rows[1][:], by_customer[1])
-        nc.sync.dma_start(offsets[:], offs)
-        nc.sync.dma_start(left[:], w_left)
+        nc.scalar.dma_start(left[:], w_left)
+        nc.sync.dma_start(rows[1][:], by_customer[1])
         nc.scalar.dma_start(right[:], w_right)
-        nc.scalar.dma_start(vectors[0:U_BLOCKS, :], b_comb.rearrange("(j p) o -> j (p o)", p=P))
-        nc.scalar.dma_start(vectors[GAIN : GAIN + 1, :], norm_w.rearrange("p o -> o p"))
-        nc.scalar.dma_start(vectors[BIAS : BIAS + 1, :], norm_b.rearrange("p o -> o p"))
+        nc.sync.dma_start(offsets[:], offs)
         comb_f32, ff_f32 = [], []
         for c in range(CHUNKS):
             span = slice(c * CHUNK * P, (c + 1) * CHUNK * P)
@@ -53,6 +52,10 @@ def tile_messagepassinglayer_b_kernel(
             nc.sync.dma_start(comb_f32[c][:], w_comb[:, span].rearrange("(k p) u -> p k u", p=P))
             ff_f32.append(held.tile([P, CHUNK, P], F32, name=f"ff_f32_{c}"))
             nc.sync.dma_start(ff_f32[c][:], w_ff[span, :].rearrange("(j p) c -> p j c", p=P))
+            if c == 0:
+                nc.sync.dma_start(vectors[0:U_BLOCKS, :], b_comb.rearrange("(j p) o -> j (p o)", p=P))
+                nc.sync.dma_start(vectors[GAIN : GAIN + 1, :], norm_w.rearrange("p o -> o p"))
+                nc.sync.dma_start(vectors[BIAS : BIAS + 1, :], norm_b.rearrange("p o -> o p"))
 
         identity = held.tile([P, P], BF16, name="identity")
         masks.make_identity(nc, identity[:])
@@ -60,31 +63,33 @@ def tile_messagepassinglayer_b_kernel(
         masks.make_identity(nc, identity_f32[:])
         eps = held.tile([P, 1], F32, name="eps")
         nc.vector.memset(eps[:], EPS)
+        warm = held.tile([P, 1], F32, name="warm")
+        nc.scalar.activation(warm[:], eps[:], ACT.Abs_reciprocal_sqrt)
 
         window = [held.tile([P, S], BF16, name=f"window{b}") for b in range(B)]
         for b in range(B):
-            turned = work.tile([P, S], BF16, tag="work", name="turned")
-            for a in range(S // P):
-                nc.tensor.transpose(turned[:, a * P : (a + 1) * P], rows[b][:, a, :], identity[:])
-            if b == 0:
-                nc.vector.tensor_copy(window[b][:], turned[:])
-            else:
-                nc.scalar.copy(window[b][:], turned[:])
-
-        columns_psum = work.tile([P, VECTOR_ROWS], F32, tag="work", name="columns_psum")
-        nc.tensor.transpose(columns_psum[:], vectors[:], identity_f32[:])
-        columns = held.tile([P, VECTOR_ROWS], F32, name="columns")
-        nc.vector.tensor_copy(columns[:], columns_psum[:])
+            turned = work.tile([P, ROWS, P], BF16, tag="work", name="turned")
+            for a in range(ROWS):
+                nc.tensor.transpose(turned[:, a, :], rows[b][:, a, :], identity[:])
+            in_order = turned[:].rearrange("d a p -> d p a")
+            columns_of = window[b][:].rearrange("d (p a) -> d p a", a=ROWS)
+            nc.scalar.copy(columns_of, in_order)
 
         comb, ff = {}, {}
 
-        def round_chunk(c):
-            comb[c] = held.tile([P, K_BLOCKS, CHUNK * P], BF16, name=f"comb{c}")
-            nc.vector.tensor_copy(comb[c][:], comb_f32[c][:])
-            ff[c] = held.tile([P, CHUNK, P], BF16, name=f"ff{c}")
-            nc.scalar.copy(ff[c][:], ff_f32[c][:])
+        def round_comb(u):
+            c, j = divmod(u, CHUNK)
+            comb[u] = held.tile([P, K_BLOCKS, P], BF16, name=f"comb{u}")
+            nc.vector.tensor_copy(comb[u][:], comb_f32[c][:, :, j * P : (j + 1) * P])
 
-        round_chunk(0)
+        def round_ff(u):
+            c, j = divmod(u, CHUNK)
+            ff[u] = held.tile([P, P], BF16, name=f"ff{u}")
+            nc.vector.tensor_copy(ff[u][:], ff_f32[c][:, j, :])
+
+        for u in range(AHEAD):
+            round_comb(u)
+            round_ff(u)
 
         info = [[held.tile([P, S], BF16, name=f"info{b}_{m}") for m in range(M_BLOCKS)] for b in range(B)]
         for b in range(B):
@@ -100,23 +105,23 @@ def tile_messagepassinglayer_b_kernel(
                             start=side == 0,
                             stop=side == 1,
                         )
-                    rounded = info[b][m][:, h * HALF : (h + 1) * HALF]
-                    if m == 0:
-                        nc.scalar.copy(rounded, both[:])
-                    else:
-                        nc.vector.tensor_copy(rounded, both[:])
+                    nc.scalar.copy(info[b][m][:, h * HALF : (h + 1) * HALF], both[:])
+
+        columns_psum = work.tile([P, VECTOR_ROWS], F32, tag="work", name="columns_psum")
+        nc.tensor.transpose(columns_psum[:], vectors[:], identity_f32[:])
+        columns = held.tile([P, VECTOR_ROWS], F32, name="columns")
+        nc.vector.tensor_copy(columns[:], columns_psum[:])
 
         added = [[sums.tile([P, HALF], F32, name=f"added{b}_{h}") for h in range(2)] for b in range(B)]
 
         def hidden_block(b, u):
-            c, j = divmod(u, CHUNK)
             moving = (window[b], info[b][0], info[b][1])
             pre = [work.tile([P, HALF], F32, tag="work", name=f"pre{h}") for h in range(2)]
-            for k in range(K_BLOCKS):
-                for h in range(2):
+            for h in range(2):
+                for k in range(K_BLOCKS):
                     nc.tensor.matmul(
                         pre[h][:],
-                        comb[c][:, k, j * P : (j + 1) * P],
+                        comb[u][:, k, :],
                         moving[k][:, h * HALF : (h + 1) * HALF],
                         start=k == 0,
                         stop=k == K_BLOCKS - 1,
@@ -127,9 +132,8 @@ def tile_messagepassinglayer_b_kernel(
             return hid
 
         def feed_forward(b, u, hid):
-            c, j = divmod(u, CHUNK)
             for h in range(2):
-                nc.tensor.matmul(added[b][h][:], ff[c][:, j, :], hid[h][:], start=False, stop=u == U_BLOCKS - 1)
+                nc.tensor.matmul(added[b][h][:], ff[u][:], hid[h][:], start=False, stop=u == U_BLOCKS - 1)
             if u == U_BLOCKS - 1:
                 normalise(b)
 
@@ -139,14 +143,15 @@ def tile_messagepassinglayer_b_kernel(
                 nc.vector.bn_stats(stats[:, 6 * h : 6 * h + 6], added[b][h][:])
             mean_var = ring.tile([P, 2], F32, name="mean_var")
             nc.vector.bn_aggr(mean_var[:], stats[:])
-            std = ring.tile([P, 1], F32, name="std")
-            nc.scalar.activation(std[:], mean_var[:, 1:2], ACT.Sqrt, bias=eps[:])
+            norm_w_column, norm_b_column = columns[:, GAIN : GAIN + 1], columns[:, BIAS : BIAS + 1]
+            inv_std = ring.tile([P, 1], F32, name="inv_std")
+            nc.scalar.activation(inv_std[:], mean_var[:, 1:2], ACT.Abs_reciprocal_sqrt, bias=eps[:])
+            minus_mean_w = ring.tile([P, 1], F32, name="minus_mean_w")
+            nc.vector.tensor_scalar(minus_mean_w[:], mean_var[:, 0:1], norm_w_column, -1.0, op0=ALU.mult, op1=ALU.mult)
             gain = ring.tile([P, 1], F32, name="gain")
-            nc.vector.reciprocal(gain[:], std[:])
-            nc.vector.tensor_mul(gain[:], gain[:], columns[:, GAIN : GAIN + 1])
+            nc.vector.tensor_mul(gain[:], inv_std[:], norm_w_column)
             shift = ring.tile([P, 1], F32, name="shift")
-            nc.vector.tensor_mul(shift[:], mean_var[:, 0:1], gain[:])
-            nc.vector.tensor_sub(shift[:], columns[:, BIAS : BIAS + 1], shift[:])
+            nc.vector.tensor_scalar(shift[:], inv_std[:], minus_mean_w[:], norm_b_column, op0=ALU.mult, op1=ALU.add)
             normed = [ring.tile([P, HALF], F32, name=f"normed{h}") for h in range(2)]
             nc.scalar.activation(normed[0][:], added[b][0][:], ACT.Identity, bias=shift[:], scale=gain[:])
             nc.vector.tensor_scalar(normed[1][:], added[b][1][:], gain[:], shift[:], op0=ALU.mult, op1=ALU.add)
@@ -160,10 +165,11 @@ def tile_messagepassinglayer_b_kernel(
                     added[b][h][:], identity[:], window[b][:, h * HALF : (h + 1) * HALF], start=True, stop=False
                 )
             for u in range(U_BLOCKS):
-                if b == 0 and u % CHUNK == 0 and u // CHUNK + 1 < CHUNKS:
-                    round_chunk(u // CHUNK + 1)
                 hid = hidden_block(b, u)
                 if waiting is not None:
                     feed_forward(*waiting)
                 waiting = (b, u, hid)
+                if b == 0 and u + AHEAD < U_BLOCKS:
+                    round_comb(u + AHEAD)
+                    round_ff(u + AHEAD)
         feed_forward(*waiting)

@@ -17,6 +17,9 @@ U_BLOCKS = U // P
 CHUNK = 4
 CHUNKS = U_BLOCKS // CHUNK
 AHEAD = 4
+PIECE = 512
+PIECES = B * S // PIECE
+LAG = 2
 VECTOR_ROWS = 64
 GAIN, BIAS = U_BLOCKS, U_BLOCKS + 1
 
@@ -29,7 +32,8 @@ def tile_messagepassinglayer_b_kernel(
     nc = tc.nc
     with (
         tc.tile_pool(name="held", bufs=1) as held,
-        tc.tile_pool(name="ring", bufs=3) as ring,
+        tc.tile_pool(name="ring", bufs=2) as ring,
+        tc.tile_pool(name="hids", bufs=LAG + 2) as hids,
         tc.psum_pool(name="sums", bufs=1) as sums,
         tc.psum_pool(name="work", bufs=4) as work,
     ):
@@ -75,6 +79,10 @@ def tile_messagepassinglayer_b_kernel(
             columns_of = window[b][:].rearrange("d (p a) -> d p a", a=ROWS)
             nc.scalar.copy(columns_of, in_order)
 
+        own = held.tile([P, B * S], BF16, name="own")
+        for b in range(B):
+            nc.vector.tensor_copy(own[:, b * S : (b + 1) * S], window[b][:])
+
         comb, ff = {}, {}
 
         def round_comb(u):
@@ -91,7 +99,7 @@ def tile_messagepassinglayer_b_kernel(
             round_comb(u)
             round_ff(u)
 
-        info = [[held.tile([P, S], BF16, name=f"info{b}_{m}") for m in range(M_BLOCKS)] for b in range(B)]
+        info = [held.tile([P, B * S], BF16, name=f"info{m}") for m in range(M_BLOCKS)]
         for b in range(B):
             for h in range(2):
                 for m in range(M_BLOCKS):
@@ -105,44 +113,53 @@ def tile_messagepassinglayer_b_kernel(
                             start=side == 0,
                             stop=side == 1,
                         )
-                    nc.scalar.copy(info[b][m][:, h * HALF : (h + 1) * HALF], both[:])
+                    nc.scalar.copy(info[m][:, b * S + h * HALF : b * S + (h + 1) * HALF], both[:])
 
         columns_psum = work.tile([P, VECTOR_ROWS], F32, tag="work", name="columns_psum")
         nc.tensor.transpose(columns_psum[:], vectors[:], identity_f32[:])
         columns = held.tile([P, VECTOR_ROWS], F32, name="columns")
         nc.vector.tensor_copy(columns[:], columns_psum[:])
 
-        added = [[sums.tile([P, HALF], F32, name=f"added{b}_{h}") for h in range(2)] for b in range(B)]
+        added = [sums.tile([P, PIECE], F32, name=f"added{q}") for q in range(PIECES)]
+        moving = (own, info[0], info[1])
+        parts = [[] for b in range(B)]
+        for q in range(PIECES):
+            for b in range(B):
+                lo, hi = max(q * PIECE, b * S), min((q + 1) * PIECE, (b + 1) * S)
+                if lo < hi:
+                    parts[b].append((q, lo - q * PIECE, hi - q * PIECE, lo))
+        stats = [held.tile([P, len(parts[b]), 6], F32, name=f"stats{b}") for b in range(B)]
 
-        def hidden_block(b, u):
-            moving = (window[b], info[b][0], info[b][1])
-            pre = [work.tile([P, HALF], F32, tag="work", name=f"pre{h}") for h in range(2)]
-            for h in range(2):
-                for k in range(K_BLOCKS):
-                    nc.tensor.matmul(
-                        pre[h][:],
-                        comb[u][:, k, :],
-                        moving[k][:, h * HALF : (h + 1) * HALF],
-                        start=k == 0,
-                        stop=k == K_BLOCKS - 1,
-                    )
-            hid = [ring.tile([P, HALF], BF16, name=f"hid{h}") for h in range(2)]
-            nc.scalar.activation(hid[0][:], pre[0][:], ACT.Relu, bias=columns[:, u : u + 1])
-            nc.vector.tensor_scalar(hid[1][:], pre[1][:], columns[:, u : u + 1], 0.0, op0=ALU.add, op1=ALU.max)
+        def hidden_block(q, u):
+            pre = work.tile([P, PIECE], F32, tag="work", name="pre")
+            for k in range(K_BLOCKS):
+                nc.tensor.matmul(
+                    pre[:],
+                    comb[u][:, k, :],
+                    moving[k][:, q * PIECE : (q + 1) * PIECE],
+                    start=k == 0,
+                    stop=k == K_BLOCKS - 1,
+                )
+            hid = hids.tile([P, PIECE], BF16, name="hid")
+            if u % 2 == 0:
+                nc.scalar.activation(hid[:], pre[:], ACT.Relu, bias=columns[:, u : u + 1])
+            else:
+                nc.vector.tensor_scalar(hid[:], pre[:], columns[:, u : u + 1], 0.0, op0=ALU.add, op1=ALU.max)
             return hid
 
-        def feed_forward(b, u, hid):
-            for h in range(2):
-                nc.tensor.matmul(added[b][h][:], ff[u][:], hid[h][:], start=False, stop=u == U_BLOCKS - 1)
+        def feed_forward(q, u, hid):
+            nc.tensor.matmul(added[q][:], ff[u][:], hid[:], start=False, stop=u == U_BLOCKS - 1)
             if u == U_BLOCKS - 1:
-                normalise(b)
+                for b in range(B):
+                    for i, (piece, lo, hi, first) in enumerate(parts[b]):
+                        if piece == q:
+                            nc.vector.bn_stats(stats[b][:, i, :], added[q][:, lo:hi])
+                            if i == len(parts[b]) - 1:
+                                normalise(b)
 
         def normalise(b):
-            stats = ring.tile([P, 2 * 6], F32, name="stats")
-            for h in range(2):
-                nc.vector.bn_stats(stats[:, 6 * h : 6 * h + 6], added[b][h][:])
             mean_var = ring.tile([P, 2], F32, name="mean_var")
-            nc.vector.bn_aggr(mean_var[:], stats[:])
+            nc.vector.bn_aggr(mean_var[:], stats[b][:].rearrange("p i s -> p (i s)"))
             norm_w_column, norm_b_column = columns[:, GAIN : GAIN + 1], columns[:, BIAS : BIAS + 1]
             inv_std = ring.tile([P, 1], F32, name="inv_std")
             nc.scalar.activation(inv_std[:], mean_var[:, 1:2], ACT.Abs_reciprocal_sqrt, bias=eps[:])
@@ -152,24 +169,24 @@ def tile_messagepassinglayer_b_kernel(
             nc.vector.tensor_mul(gain[:], inv_std[:], norm_w_column)
             shift = ring.tile([P, 1], F32, name="shift")
             nc.vector.tensor_scalar(shift[:], inv_std[:], minus_mean_w[:], norm_b_column, op0=ALU.mult, op1=ALU.add)
-            normed = [ring.tile([P, HALF], F32, name=f"normed{h}") for h in range(2)]
-            nc.scalar.activation(normed[0][:], added[b][0][:], ACT.Identity, bias=shift[:], scale=gain[:])
-            nc.vector.tensor_scalar(normed[1][:], added[b][1][:], gain[:], shift[:], op0=ALU.mult, op1=ALU.add)
-            nc.scalar.dma_start(out[:, b * S : b * S + HALF], normed[0][:])
-            nc.sync.dma_start(out[:, b * S + HALF : (b + 1) * S], normed[1][:])
+            for i, (q, lo, hi, first) in enumerate(parts[b]):
+                normed = ring.tile([P, hi - lo], F32, name=f"normed{i}")
+                if i % 2 == 0:
+                    nc.vector.tensor_scalar(normed[:], added[q][:, lo:hi], gain[:], shift[:], op0=ALU.mult, op1=ALU.add)
+                    nc.sync.dma_start(out[:, first : first + hi - lo], normed[:])
+                else:
+                    nc.scalar.activation(normed[:], added[q][:, lo:hi], ACT.Identity, bias=shift[:], scale=gain[:])
+                    nc.scalar.dma_start(out[:, first : first + hi - lo], normed[:])
 
-        waiting = None
-        for b in range(B):
-            for h in range(2):
-                nc.tensor.matmul(
-                    added[b][h][:], identity[:], window[b][:, h * HALF : (h + 1) * HALF], start=True, stop=False
-                )
+        waiting = []
+        for q in range(PIECES):
+            nc.tensor.matmul(added[q][:], identity[:], own[:, q * PIECE : (q + 1) * PIECE], start=True, stop=False)
             for u in range(U_BLOCKS):
-                hid = hidden_block(b, u)
-                if waiting is not None:
-                    feed_forward(*waiting)
-                waiting = (b, u, hid)
-                if b == 0 and u + AHEAD < U_BLOCKS:
+                waiting.append((q, u, hidden_block(q, u)))
+                if len(waiting) > LAG:
+                    feed_forward(*waiting.pop(0))
+                if q == 0 and u + AHEAD < U_BLOCKS:
                     round_comb(u + AHEAD)
                     round_ff(u + AHEAD)
-        feed_forward(*waiting)
+        for late in waiting:
+            feed_forward(*late)

@@ -9,7 +9,9 @@ P = 128
 B, S = 2, 768
 M, U = 256, 4096
 EPS = 1e-5
-ROWS = S // P
+GROUPS = 3
+GROUP = S // GROUPS
+ROWS = GROUP // P
 HALF = S // 2
 M_BLOCKS = M // P
 K_BLOCKS = 1 + M_BLOCKS
@@ -19,9 +21,8 @@ CHUNKS = U_BLOCKS // CHUNK
 AHEAD = 4
 PIECE = 512
 PIECES = B * S // PIECE
-LAG = 2
-VECTOR_ROWS = 64
-GAIN, BIAS = U_BLOCKS, U_BLOCKS + 1
+LAST = PIECES - 1
+LAG = 5
 
 FLOPS = 2 * B * S * (2 * P * M + (P + M) * U + U * P)
 
@@ -37,13 +38,14 @@ def tile_messagepassinglayer_b_kernel(
         tc.psum_pool(name="sums", bufs=1) as sums,
         tc.psum_pool(name="work", bufs=4) as work,
     ):
-        rows = [held.tile([P, ROWS, P], BF16, name=f"rows{b}") for b in range(B)]
+        rows = [held.tile([P, GROUPS, ROWS, P], BF16, name=f"rows{b}") for b in range(B)]
         offsets = held.tile([P, B * 2 * S // 16], U16, name="offsets")
         left = held.tile([P, M], BF16, name="left")
         right = held.tile([P, M], BF16, name="right")
-        vectors = held.tile([VECTOR_ROWS, P], F32, name="vectors")
-        by_customer = table.rearrange("b (p a) d -> b p a d", a=ROWS)
-        nc.vector.memset(vectors[:], 0.0)
+        bias = held.tile([P, U_BLOCKS], F32, name="bias")
+        norm_w_column = held.tile([P, 1], F32, name="norm_w_column")
+        norm_b_column = held.tile([P, 1], F32, name="norm_b_column")
+        by_customer = table.rearrange("b (g p a) d -> b p g a d", g=GROUPS, a=ROWS)
         nc.sync.dma_start(rows[0][:], by_customer[0])
         nc.scalar.dma_start(left[:], w_left)
         nc.sync.dma_start(rows[1][:], by_customer[1])
@@ -57,14 +59,12 @@ def tile_messagepassinglayer_b_kernel(
             ff_f32.append(held.tile([P, CHUNK, P], F32, name=f"ff_f32_{c}"))
             nc.sync.dma_start(ff_f32[c][:], w_ff[span, :].rearrange("(j p) c -> p j c", p=P))
             if c == 0:
-                nc.sync.dma_start(vectors[0:U_BLOCKS, :], b_comb.rearrange("(j p) o -> j (p o)", p=P))
-                nc.sync.dma_start(vectors[GAIN : GAIN + 1, :], norm_w.rearrange("p o -> o p"))
-                nc.sync.dma_start(vectors[BIAS : BIAS + 1, :], norm_b.rearrange("p o -> o p"))
+                nc.sync.dma_start(bias[:], b_comb.rearrange("(j p) o -> p (j o)", p=P))
+        nc.sync.dma_start(norm_w_column[:], norm_w)
+        nc.sync.dma_start(norm_b_column[:], norm_b)
 
         identity = held.tile([P, P], BF16, name="identity")
         masks.make_identity(nc, identity[:])
-        identity_f32 = held.tile([VECTOR_ROWS, VECTOR_ROWS], F32, name="identity_f32")
-        masks.make_identity(nc, identity_f32[:])
         eps = held.tile([P, 1], F32, name="eps")
         nc.vector.memset(eps[:], EPS)
         warm = held.tile([P, 1], F32, name="warm")
@@ -72,12 +72,13 @@ def tile_messagepassinglayer_b_kernel(
 
         window = [held.tile([P, S], BF16, name=f"window{b}") for b in range(B)]
         for b in range(B):
-            turned = work.tile([P, ROWS, P], BF16, tag="work", name="turned")
-            for a in range(ROWS):
-                nc.tensor.transpose(turned[:, a, :], rows[b][:, a, :], identity[:])
-            in_order = turned[:].rearrange("d a p -> d p a")
-            columns_of = window[b][:].rearrange("d (p a) -> d p a", a=ROWS)
-            nc.scalar.copy(columns_of, in_order)
+            for g in range(GROUPS):
+                turned = work.tile([P, ROWS, P], BF16, tag="work", name="turned")
+                for a in range(ROWS):
+                    nc.tensor.transpose(turned[:, a, :], rows[b][:, g, a, :], identity[:])
+                in_order = turned[:].rearrange("d a p -> d p a")
+                columns_of = window[b][:, g * GROUP : (g + 1) * GROUP].rearrange("d (p a) -> d p a", a=ROWS)
+                nc.scalar.copy(columns_of, in_order)
 
         own = held.tile([P, B * S], BF16, name="own")
         for b in range(B):
@@ -115,12 +116,8 @@ def tile_messagepassinglayer_b_kernel(
                         )
                     nc.scalar.copy(info[m][:, b * S + h * HALF : b * S + (h + 1) * HALF], both[:])
 
-        columns_psum = work.tile([P, VECTOR_ROWS], F32, tag="work", name="columns_psum")
-        nc.tensor.transpose(columns_psum[:], vectors[:], identity_f32[:])
-        columns = held.tile([P, VECTOR_ROWS], F32, name="columns")
-        nc.vector.tensor_copy(columns[:], columns_psum[:])
-
-        added = [sums.tile([P, PIECE], F32, name=f"added{q}") for q in range(PIECES)]
+        product = [sums.tile([P, PIECE], F32, name=f"product{q}") for q in range(PIECES)]
+        added = {LAST: product[LAST]}
         moving = (own, info[0], info[1])
         parts = [[] for b in range(B)]
         for q in range(PIECES):
@@ -142,14 +139,17 @@ def tile_messagepassinglayer_b_kernel(
                 )
             hid = hids.tile([P, PIECE], BF16, name="hid")
             if u % 2 == 0:
-                nc.scalar.activation(hid[:], pre[:], ACT.Relu, bias=columns[:, u : u + 1])
+                nc.scalar.activation(hid[:], pre[:], ACT.Relu, bias=bias[:, u : u + 1])
             else:
-                nc.vector.tensor_scalar(hid[:], pre[:], columns[:, u : u + 1], 0.0, op0=ALU.add, op1=ALU.max)
+                nc.vector.tensor_scalar(hid[:], pre[:], bias[:, u : u + 1], 0.0, op0=ALU.add, op1=ALU.max)
             return hid
 
         def feed_forward(q, u, hid):
-            nc.tensor.matmul(added[q][:], ff[u][:], hid[:], start=False, stop=u == U_BLOCKS - 1)
+            nc.tensor.matmul(product[q][:], ff[u][:], hid[:], start=u == 0 and q != LAST, stop=u == U_BLOCKS - 1)
             if u == U_BLOCKS - 1:
+                if q != LAST:
+                    added[q] = held.tile([P, PIECE], F32, name=f"added{q}")
+                    nc.vector.tensor_add(added[q][:], product[q][:], own[:, q * PIECE : (q + 1) * PIECE])
                 for b in range(B):
                     for i, (piece, lo, hi, first) in enumerate(parts[b]):
                         if piece == q:
@@ -160,15 +160,14 @@ def tile_messagepassinglayer_b_kernel(
         def normalise(b):
             mean_var = ring.tile([P, 2], F32, name="mean_var")
             nc.vector.bn_aggr(mean_var[:], stats[b][:].rearrange("p i s -> p (i s)"))
-            norm_w_column, norm_b_column = columns[:, GAIN : GAIN + 1], columns[:, BIAS : BIAS + 1]
             inv_std = ring.tile([P, 1], F32, name="inv_std")
             nc.scalar.activation(inv_std[:], mean_var[:, 1:2], ACT.Abs_reciprocal_sqrt, bias=eps[:])
             minus_mean_w = ring.tile([P, 1], F32, name="minus_mean_w")
-            nc.vector.tensor_scalar(minus_mean_w[:], mean_var[:, 0:1], norm_w_column, -1.0, op0=ALU.mult, op1=ALU.mult)
+            nc.vector.tensor_scalar(minus_mean_w[:], mean_var[:, 0:1], norm_w_column[:], -1.0, op0=ALU.mult, op1=ALU.mult)
             gain = ring.tile([P, 1], F32, name="gain")
-            nc.vector.tensor_mul(gain[:], inv_std[:], norm_w_column)
+            nc.vector.tensor_mul(gain[:], inv_std[:], norm_w_column[:])
             shift = ring.tile([P, 1], F32, name="shift")
-            nc.vector.tensor_scalar(shift[:], inv_std[:], minus_mean_w[:], norm_b_column, op0=ALU.mult, op1=ALU.add)
+            nc.vector.tensor_scalar(shift[:], inv_std[:], minus_mean_w[:], norm_b_column[:], op0=ALU.mult, op1=ALU.add)
             for i, (q, lo, hi, first) in enumerate(parts[b]):
                 normed = ring.tile([P, hi - lo], F32, name=f"normed{i}")
                 if i % 2 == 0:
@@ -180,7 +179,8 @@ def tile_messagepassinglayer_b_kernel(
 
         waiting = []
         for q in range(PIECES):
-            nc.tensor.matmul(added[q][:], identity[:], own[:, q * PIECE : (q + 1) * PIECE], start=True, stop=False)
+            if q == LAST:
+                nc.tensor.matmul(product[q][:], identity[:], own[:, q * PIECE : (q + 1) * PIECE], start=True, stop=False)
             for u in range(U_BLOCKS):
                 waiting.append((q, u, hidden_block(q, u)))
                 if len(waiting) > LAG:

@@ -23,6 +23,8 @@ PIECE = 512
 PIECES = B * S // PIECE
 LAST = PIECES - 1
 LAG = 5
+VECTOR_ROWS = 64
+GAIN, BIAS = U_BLOCKS, U_BLOCKS + 1
 
 FLOPS = 2 * B * S * (2 * P * M + (P + M) * U + U * P)
 
@@ -42,10 +44,9 @@ def tile_messagepassinglayer_b_kernel(
         offsets = held.tile([P, B * 2 * S // 16], U16, name="offsets")
         left = held.tile([P, M], BF16, name="left")
         right = held.tile([P, M], BF16, name="right")
-        bias = held.tile([P, U_BLOCKS], F32, name="bias")
-        norm_w_column = held.tile([P, 1], F32, name="norm_w_column")
-        norm_b_column = held.tile([P, 1], F32, name="norm_b_column")
+        vectors = held.tile([VECTOR_ROWS, P], F32, name="vectors")
         by_customer = table.rearrange("b (g p a) d -> b p g a d", g=GROUPS, a=ROWS)
+        nc.vector.memset(vectors[:], 0.0)
         nc.sync.dma_start(rows[0][:], by_customer[0])
         nc.scalar.dma_start(left[:], w_left)
         nc.sync.dma_start(rows[1][:], by_customer[1])
@@ -59,12 +60,14 @@ def tile_messagepassinglayer_b_kernel(
             ff_f32.append(held.tile([P, CHUNK, P], F32, name=f"ff_f32_{c}"))
             nc.sync.dma_start(ff_f32[c][:], w_ff[span, :].rearrange("(j p) c -> p j c", p=P))
             if c == 0:
-                nc.sync.dma_start(bias[:], b_comb.rearrange("(j p) o -> p (j o)", p=P))
-        nc.sync.dma_start(norm_w_column[:], norm_w)
-        nc.sync.dma_start(norm_b_column[:], norm_b)
+                nc.sync.dma_start(vectors[0:U_BLOCKS, :], b_comb.rearrange("(j p) o -> j (p o)", p=P))
+                nc.sync.dma_start(vectors[GAIN : GAIN + 1, :], norm_w.rearrange("p o -> o p"))
+                nc.sync.dma_start(vectors[BIAS : BIAS + 1, :], norm_b.rearrange("p o -> o p"))
 
         identity = held.tile([P, P], BF16, name="identity")
         masks.make_identity(nc, identity[:])
+        identity_f32 = held.tile([VECTOR_ROWS, VECTOR_ROWS], F32, name="identity_f32")
+        masks.make_identity(nc, identity_f32[:])
         eps = held.tile([P, 1], F32, name="eps")
         nc.vector.memset(eps[:], EPS)
         warm = held.tile([P, 1], F32, name="warm")
@@ -116,6 +119,11 @@ def tile_messagepassinglayer_b_kernel(
                         )
                     nc.scalar.copy(info[m][:, b * S + h * HALF : b * S + (h + 1) * HALF], both[:])
 
+        columns_psum = work.tile([P, VECTOR_ROWS], F32, tag="work", name="columns_psum")
+        nc.tensor.transpose(columns_psum[:], vectors[:], identity_f32[:])
+        columns = held.tile([P, VECTOR_ROWS], F32, name="columns")
+        nc.vector.tensor_copy(columns[:], columns_psum[:])
+
         product = [sums.tile([P, PIECE], F32, name=f"product{q}") for q in range(PIECES)]
         added = {LAST: product[LAST]}
         moving = (own, info[0], info[1])
@@ -139,9 +147,9 @@ def tile_messagepassinglayer_b_kernel(
                 )
             hid = hids.tile([P, PIECE], BF16, name="hid")
             if u % 2 == 0:
-                nc.scalar.activation(hid[:], pre[:], ACT.Relu, bias=bias[:, u : u + 1])
+                nc.scalar.activation(hid[:], pre[:], ACT.Relu, bias=columns[:, u : u + 1])
             else:
-                nc.vector.tensor_scalar(hid[:], pre[:], bias[:, u : u + 1], 0.0, op0=ALU.add, op1=ALU.max)
+                nc.vector.tensor_scalar(hid[:], pre[:], columns[:, u : u + 1], 0.0, op0=ALU.add, op1=ALU.max)
             return hid
 
         def feed_forward(q, u, hid):
@@ -160,14 +168,15 @@ def tile_messagepassinglayer_b_kernel(
         def normalise(b):
             mean_var = ring.tile([P, 2], F32, name="mean_var")
             nc.vector.bn_aggr(mean_var[:], stats[b][:].rearrange("p i s -> p (i s)"))
+            norm_w_column, norm_b_column = columns[:, GAIN : GAIN + 1], columns[:, BIAS : BIAS + 1]
             inv_std = ring.tile([P, 1], F32, name="inv_std")
             nc.scalar.activation(inv_std[:], mean_var[:, 1:2], ACT.Abs_reciprocal_sqrt, bias=eps[:])
             minus_mean_w = ring.tile([P, 1], F32, name="minus_mean_w")
-            nc.vector.tensor_scalar(minus_mean_w[:], mean_var[:, 0:1], norm_w_column[:], -1.0, op0=ALU.mult, op1=ALU.mult)
+            nc.vector.tensor_scalar(minus_mean_w[:], mean_var[:, 0:1], norm_w_column, -1.0, op0=ALU.mult, op1=ALU.mult)
             gain = ring.tile([P, 1], F32, name="gain")
-            nc.vector.tensor_mul(gain[:], inv_std[:], norm_w_column[:])
+            nc.vector.tensor_mul(gain[:], inv_std[:], norm_w_column)
             shift = ring.tile([P, 1], F32, name="shift")
-            nc.vector.tensor_scalar(shift[:], inv_std[:], minus_mean_w[:], norm_b_column[:], op0=ALU.mult, op1=ALU.add)
+            nc.vector.tensor_scalar(shift[:], inv_std[:], minus_mean_w[:], norm_b_column, op0=ALU.mult, op1=ALU.add)
             for i, (q, lo, hi, first) in enumerate(parts[b]):
                 normed = ring.tile([P, hi - lo], F32, name=f"normed{i}")
                 if i % 2 == 0:

@@ -47,7 +47,8 @@ def tile_messagepassinglayer_b_kernel(
         vectors = held.tile([VECTOR_ROWS, P], F32, name="vectors")
         by_customer = table.rearrange("b (g p a) d -> b p g a d", g=GROUPS, a=ROWS)
         nc.vector.memset(vectors[:], 0.0)
-        nc.sync.dma_start(rows[0][:], by_customer[0])
+        for g in range(GROUPS):
+            nc.sync.dma_start(rows[0][:, g], by_customer[0][:, g])
         nc.scalar.dma_start(left[:], w_left)
         nc.sync.dma_start(rows[1][:], by_customer[1])
         nc.scalar.dma_start(right[:], w_right)

@@ -23,7 +23,7 @@ PIECE = 512
 PIECES = B * S // PIECE
 LAST = PIECES - 1
 LAG = 5
-VECTOR_ROWS = 64
+VECTOR_ROWS = 128
 GAIN, BIAS = U_BLOCKS, U_BLOCKS + 1
 
 FLOPS = 2 * B * S * (2 * P * M + (P + M) * U + U * P)

@@ -49,10 +49,10 @@ def tile_messagepassinglayer_b_kernel(
         nc.vector.memset(vectors[:], 0.0)
         for g in range(GROUPS):
             nc.sync.dma_start(rows[0][:, g], by_customer[0][:, g])
-        nc.scalar.dma_start(left[:], w_left)
         nc.sync.dma_start(rows[1][:], by_customer[1])
-        nc.scalar.dma_start(right[:], w_right)
         nc.sync.dma_start(offsets[:], offs)
+        nc.sync.dma_start(left[:], w_left)
+        nc.sync.dma_start(right[:], w_right)
         comb_f32, ff_f32 = [], []
         for c in range(CHUNKS):
             span = slice(c * CHUNK * P, (c + 1) * CHUNK * P)

@@ -185,7 +185,7 @@ def tile_messagepassinglayer_b_kernel(
                     nc.sync.dma_start(out[:, first : first + hi - lo], normed[:])
                 else:
                     nc.scalar.activation(normed[:], added[q][:, lo:hi], ACT.Identity, bias=shift[:], scale=gain[:])
-                    nc.scalar.dma_start(out[:, first : first + hi - lo], normed[:])
+                    nc.sync.dma_start(out[:, first : first + hi - lo], normed[:])
 
         waiting = []
         for q in range(PIECES):

@@ -18,13 +18,10 @@ K_BLOCKS = 1 + M_BLOCKS
 U_BLOCKS = U // P
 CHUNK = 4
 CHUNKS = U_BLOCKS // CHUNK
-AHEAD = 4
 PIECE = 512
 PIECES = B * S // PIECE
 LAST = PIECES - 1
 LAG = 5
-VECTOR_ROWS = 128
-GAIN, BIAS = U_BLOCKS, U_BLOCKS + 1
 
 FLOPS = 2 * B * S * (2 * P * M + (P + M) * U + U * P)
 
@@ -44,9 +41,10 @@ def tile_messagepassinglayer_b_kernel(
         offsets = held.tile([P, B * 2 * S // 16], U16, name="offsets")
         left = held.tile([P, M], BF16, name="left")
         right = held.tile([P, M], BF16, name="right")
-        vectors = held.tile([VECTOR_ROWS, P], F32, name="vectors")
+        bias = held.tile([P, CHUNKS, CHUNK], F32, name="bias")
+        norm_w_column = held.tile([P, 1], F32, name="norm_w_column")
+        norm_b_column = held.tile([P, 1], F32, name="norm_b_column")
         by_customer = table.rearrange("b (g p a) d -> b p g a d", g=GROUPS, a=ROWS)
-        nc.vector.memset(vectors[:], 0.0)
         for g in range(GROUPS):
             nc.sync.dma_start(rows[0][:, g], by_customer[0][:, g])
         nc.sync.dma_start(rows[1][:], by_customer[1])
@@ -59,16 +57,14 @@ def tile_messagepassinglayer_b_kernel(
             comb_f32.append(held.tile([P, K_BLOCKS, CHUNK * P], F32, name=f"comb_f32_{c}"))
             nc.sync.dma_start(comb_f32[c][:], w_comb[:, span].rearrange("(k p) u -> p k u", p=P))
             ff_f32.append(held.tile([P, CHUNK, P], F32, name=f"ff_f32_{c}"))
-            nc.sync.dma_start(ff_f32[c][:], w_ff[span, :].rearrange("(j p) c -> p j c", p=P))
+            nc.sync.dma_start(ff_f32[c][:], w_ff[span, :].rearrange("(p j) c -> p j c", j=CHUNK))
             if c == 0:
-                nc.sync.dma_start(vectors[0:U_BLOCKS, :], b_comb.rearrange("(j p) o -> j (p o)", p=P))
-                nc.sync.dma_start(vectors[GAIN : GAIN + 1, :], norm_w.rearrange("p o -> o p"))
-                nc.sync.dma_start(vectors[BIAS : BIAS + 1, :], norm_b.rearrange("p o -> o p"))
+                nc.sync.dma_start(bias[:], b_comb.rearrange("(c p j) o -> p c (j o)", p=P, j=CHUNK))
+        nc.sync.dma_start(norm_w_column[:], norm_w)
+        nc.sync.dma_start(norm_b_column[:], norm_b)
 
         identity = held.tile([P, P], BF16, name="identity")
         masks.make_identity(nc, identity[:])
-        identity_f32 = held.tile([VECTOR_ROWS, VECTOR_ROWS], F32, name="identity_f32")
-        masks.make_identity(nc, identity_f32[:])
         eps = held.tile([P, 1], F32, name="eps")
         nc.vector.memset(eps[:], EPS)
         warm = held.tile([P, 1], F32, name="warm")
@@ -88,21 +84,17 @@ def tile_messagepassinglayer_b_kernel(
         for b in range(B):
             nc.vector.tensor_copy(own[:, b * S : (b + 1) * S], window[b][:])
 
-        comb, ff = {}, {}
+        comb = [held.tile([P, K_BLOCKS, CHUNK * P], BF16, name=f"comb{c}") for c in range(CHUNKS)]
+        ff = [held.tile([P, CHUNK, P], BF16, name=f"ff{c}") for c in range(CHUNKS)]
 
-        def round_comb(u):
-            c, j = divmod(u, CHUNK)
-            comb[u] = held.tile([P, K_BLOCKS, P], BF16, name=f"comb{u}")
-            nc.vector.tensor_copy(comb[u][:], comb_f32[c][:, :, j * P : (j + 1) * P])
+        def round_step(c, step):
+            if step < K_BLOCKS:
+                nc.vector.tensor_copy(comb[c][:, step, :], comb_f32[c][:, step, :])
+            else:
+                nc.vector.tensor_copy(ff[c][:], ff_f32[c][:])
 
-        def round_ff(u):
-            c, j = divmod(u, CHUNK)
-            ff[u] = held.tile([P, P], BF16, name=f"ff{u}")
-            nc.vector.tensor_copy(ff[u][:], ff_f32[c][:, j, :])
-
-        for u in range(AHEAD):
-            round_comb(u)
-            round_ff(u)
+        for step in range(CHUNK):
+            round_step(0, step)
 
         info = [held.tile([P, B * S], BF16, name=f"info{m}") for m in range(M_BLOCKS)]
         for b in range(B):
@@ -120,11 +112,6 @@ def tile_messagepassinglayer_b_kernel(
                         )
                     nc.scalar.copy(info[m][:, b * S + h * HALF : b * S + (h + 1) * HALF], both[:])
 
-        columns_psum = work.tile([P, VECTOR_ROWS], F32, tag="work", name="columns_psum")
-        nc.tensor.transpose(columns_psum[:], vectors[:], identity_f32[:])
-        columns = held.tile([P, VECTOR_ROWS], F32, name="columns")
-        nc.vector.tensor_copy(columns[:], columns_psum[:])
-
         product = [sums.tile([P, PIECE], F32, name=f"product{q}") for q in range(PIECES)]
         added = {LAST: product[LAST]}
         moving = (own, info[0], info[1])
@@ -137,24 +124,26 @@ def tile_messagepassinglayer_b_kernel(
         stats = [held.tile([P, len(parts[b]), 6], F32, name=f"stats{b}") for b in range(B)]
 
         def hidden_block(q, u):
+            c, j = divmod(u, CHUNK)
             pre = work.tile([P, PIECE], F32, tag="work", name="pre")
             for k in range(K_BLOCKS):
                 nc.tensor.matmul(
                     pre[:],
-                    comb[u][:, k, :],
+                    comb[c][:, k, :].rearrange("d (p j) -> d j p", j=CHUNK)[:, j, :],
                     moving[k][:, q * PIECE : (q + 1) * PIECE],
                     start=k == 0,
                     stop=k == K_BLOCKS - 1,
                 )
             hid = hids.tile([P, PIECE], BF16, name="hid")
             if u % 2 == 0:
-                nc.scalar.activation(hid[:], pre[:], ACT.Relu, bias=columns[:, u : u + 1])
+                nc.scalar.activation(hid[:], pre[:], ACT.Relu, bias=bias[:, c, j : j + 1])
             else:
-                nc.vector.tensor_scalar(hid[:], pre[:], columns[:, u : u + 1], 0.0, op0=ALU.add, op1=ALU.max)
+                nc.vector.tensor_scalar(hid[:], pre[:], bias[:, c, j : j + 1], 0.0, op0=ALU.add, op1=ALU.max)
             return hid
 
         def feed_forward(q, u, hid):
-            nc.tensor.matmul(product[q][:], ff[u][:], hid[:], start=u == 0 and q != LAST, stop=u == U_BLOCKS - 1)
+            c, j = divmod(u, CHUNK)
+            nc.tensor.matmul(product[q][:], ff[c][:, j, :], hid[:], start=u == 0 and q != LAST, stop=u == U_BLOCKS - 1)
             if u == U_BLOCKS - 1:
                 if q != LAST:
                     added[q] = held.tile([P, PIECE], F32, name=f"added{q}")
@@ -169,15 +158,14 @@ def tile_messagepassinglayer_b_kernel(
         def normalise(b):
             mean_var = ring.tile([P, 2], F32, name="mean_var")
             nc.vector.bn_aggr(mean_var[:], stats[b][:].rearrange("p i s -> p (i s)"))
-            norm_w_column, norm_b_column = columns[:, GAIN : GAIN + 1], columns[:, BIAS : BIAS + 1]
             inv_std = ring.tile([P, 1], F32, name="inv_std")
             nc.scalar.activation(inv_std[:], mean_var[:, 1:2], ACT.Abs_reciprocal_sqrt, bias=eps[:])
             minus_mean_w = ring.tile([P, 1], F32, name="minus_mean_w")
-            nc.vector.tensor_scalar(minus_mean_w[:], mean_var[:, 0:1], norm_w_column, -1.0, op0=ALU.mult, op1=ALU.mult)
+            nc.vector.tensor_scalar(minus_mean_w[:], mean_var[:, 0:1], norm_w_column[:], -1.0, op0=ALU.mult, op1=ALU.mult)
             gain = ring.tile([P, 1], F32, name="gain")
-            nc.vector.tensor_mul(gain[:], inv_std[:], norm_w_column)
+            nc.vector.tensor_mul(gain[:], inv_std[:], norm_w_column[:])
             shift = ring.tile([P, 1], F32, name="shift")
-            nc.vector.tensor_scalar(shift[:], inv_std[:], minus_mean_w[:], norm_b_column, op0=ALU.mult, op1=ALU.add)
+            nc.vector.tensor_scalar(shift[:], inv_std[:], minus_mean_w[:], norm_b_column[:], op0=ALU.mult, op1=ALU.add)
             for i, (q, lo, hi, first) in enumerate(parts[b]):
                 normed = ring.tile([P, hi - lo], F32, name=f"normed{i}")
                 if i % 2 == 0:
@@ -195,8 +183,7 @@ def tile_messagepassinglayer_b_kernel(
                 waiting.append((q, u, hidden_block(q, u)))
                 if len(waiting) > LAG:
                     feed_forward(*waiting.pop(0))
-                if q == 0 and u + AHEAD < U_BLOCKS:
-                    round_comb(u + AHEAD)
-                    round_ff(u + AHEAD)
+                if q == 0 and u + CHUNK < U_BLOCKS:
+                    round_step(u // CHUNK + 1, u % CHUNK)
         for late in waiting:
             feed_forward(*late)

@@ -18,10 +18,12 @@ K_BLOCKS = 1 + M_BLOCKS
 U_BLOCKS = U // P
 CHUNK = 4
 CHUNKS = U_BLOCKS // CHUNK
-PIECE = 512
-PIECES = B * S // PIECE
+BANK = 512
+WIDTHS = (BANK, BANK, BANK // 2, BANK // 2)
+STARTS = tuple(sum(WIDTHS[:q]) for q in range(len(WIDTHS)))
+PIECES = len(WIDTHS)
 LAST = PIECES - 1
-LAG = 5
+LAG = 8
 
 FLOPS = 2 * B * S * (2 * P * M + (P + M) * U + U * P)
 
@@ -112,42 +114,43 @@ def tile_messagepassinglayer_b_kernel(
                         )
                     nc.scalar.copy(info[m][:, b * S + h * HALF : b * S + (h + 1) * HALF], both[:])
 
-        product = [sums.tile([P, PIECE], F32, name=f"product{q}") for q in range(PIECES)]
+        banks = [sums.tile([P, BANK], F32, name=f"bank{q}") for q in range(PIECES)]
+        product = [banks[q][:, : WIDTHS[q]] for q in range(PIECES)]
         added = {LAST: product[LAST]}
         moving = (own, info[0], info[1])
         parts = [[] for b in range(B)]
         for q in range(PIECES):
             for b in range(B):
-                lo, hi = max(q * PIECE, b * S), min((q + 1) * PIECE, (b + 1) * S)
+                lo, hi = max(STARTS[q], b * S), min(STARTS[q] + WIDTHS[q], (b + 1) * S)
                 if lo < hi:
-                    parts[b].append((q, lo - q * PIECE, hi - q * PIECE, lo))
+                    parts[b].append((q, lo - STARTS[q], hi - STARTS[q], lo))
         stats = [held.tile([P, len(parts[b]), 6], F32, name=f"stats{b}") for b in range(B)]
 
         def hidden_block(q, u):
             c, j = divmod(u, CHUNK)
-            pre = work.tile([P, PIECE], F32, tag="work", name="pre")
+            pre = work.tile([P, WIDTHS[q]], F32, tag="work", name="pre")
             for k in range(K_BLOCKS):
                 nc.tensor.matmul(
                     pre[:],
                     comb[c][:, k, :].rearrange("d (p j) -> d j p", j=CHUNK)[:, j, :],
-                    moving[k][:, q * PIECE : (q + 1) * PIECE],
+                    moving[k][:, STARTS[q] : STARTS[q] + WIDTHS[q]],
                     start=k == 0,
                     stop=k == K_BLOCKS - 1,
                 )
-            hid = hids.tile([P, PIECE], BF16, name="hid")
+            hid = hids.tile([P, BANK], BF16, name="hid")[:, : WIDTHS[q]]
             if u % 2 == 0:
-                nc.scalar.activation(hid[:], pre[:], ACT.Relu, bias=bias[:, c, j : j + 1])
+                nc.scalar.activation(hid, pre[:], ACT.Relu, bias=bias[:, c, j : j + 1])
             else:
-                nc.vector.tensor_scalar(hid[:], pre[:], bias[:, c, j : j + 1], 0.0, op0=ALU.add, op1=ALU.max)
+                nc.vector.tensor_scalar(hid, pre[:], bias[:, c, j : j + 1], 0.0, op0=ALU.add, op1=ALU.max)
             return hid
 
         def feed_forward(q, u, hid):
             c, j = divmod(u, CHUNK)
-            nc.tensor.matmul(product[q][:], ff[c][:, j, :], hid[:], start=u == 0 and q != LAST, stop=u == U_BLOCKS - 1)
+            nc.tensor.matmul(product[q], ff[c][:, j, :], hid, start=u == 0 and q != LAST, stop=u == U_BLOCKS - 1)
             if u == U_BLOCKS - 1:
                 if q != LAST:
-                    added[q] = held.tile([P, PIECE], F32, name=f"added{q}")
-                    nc.vector.tensor_add(added[q][:], product[q][:], own[:, q * PIECE : (q + 1) * PIECE])
+                    added[q] = held.tile([P, WIDTHS[q]], F32, name=f"added{q}")[:]
+                    nc.vector.tensor_add(added[q], product[q], own[:, STARTS[q] : STARTS[q] + WIDTHS[q]])
                 for b in range(B):
                     for i, (piece, lo, hi, first) in enumerate(parts[b]):
                         if piece == q:
@@ -178,7 +181,7 @@ def tile_messagepassinglayer_b_kernel(
         waiting = []
         for q in range(PIECES):
             if q == LAST:
-                nc.tensor.matmul(product[q][:], identity[:], own[:, q * PIECE : (q + 1) * PIECE], start=True, stop=False)
+                nc.tensor.matmul(product[q], identity[:], own[:, STARTS[q] : STARTS[q] + WIDTHS[q]], start=True, stop=False)
             for u in range(U_BLOCKS):
                 waiting.append((q, u, hidden_block(q, u)))
                 if len(waiting) > LAG:

@@ -23,6 +23,14 @@ WIDTHS = (BANK, BANK, BANK // 2, BANK // 2)
 STARTS = tuple(sum(WIDTHS[:q]) for q in range(len(WIDTHS)))
 PIECES = len(WIDTHS)
 LAST = PIECES - 1
+SPLIT = 2 * CHUNK
+SWEEPS = (
+    ((0,), 0, U_BLOCKS),
+    ((1,), 0, U_BLOCKS),
+    ((2, 3), 0, U_BLOCKS - SPLIT),
+    ((2,), U_BLOCKS - SPLIT, U_BLOCKS),
+    ((3,), U_BLOCKS - SPLIT, U_BLOCKS),
+)
 LAG = 8
 
 FLOPS = 2 * B * S * (2 * P * M + (P + M) * U + U * P)
@@ -126,37 +134,49 @@ def tile_messagepassinglayer_b_kernel(
                     parts[b].append((q, lo - STARTS[q], hi - STARTS[q], lo))
         stats = [held.tile([P, len(parts[b]), 6], F32, name=f"stats{b}") for b in range(B)]
 
-        def hidden_block(q, u):
+        def hidden_block(pieces, u):
             c, j = divmod(u, CHUNK)
-            pre = work.tile([P, WIDTHS[q]], F32, tag="work", name="pre")
+            begin, width = STARTS[pieces[0]], sum(WIDTHS[q] for q in pieces)
+            pre = work.tile([P, width], F32, tag="work", name="pre")
             for k in range(K_BLOCKS):
                 nc.tensor.matmul(
                     pre[:],
                     comb[c][:, k, :].rearrange("d (p j) -> d j p", j=CHUNK)[:, j, :],
-                    moving[k][:, STARTS[q] : STARTS[q] + WIDTHS[q]],
+                    moving[k][:, begin : begin + width],
                     start=k == 0,
                     stop=k == K_BLOCKS - 1,
                 )
-            hid = hids.tile([P, BANK], BF16, name="hid")[:, : WIDTHS[q]]
+            hid = hids.tile([P, BANK], BF16, name="hid")[:, :width]
             if u % 2 == 0:
                 nc.scalar.activation(hid, pre[:], ACT.Relu, bias=bias[:, c, j : j + 1])
             else:
                 nc.vector.tensor_scalar(hid, pre[:], bias[:, c, j : j + 1], 0.0, op0=ALU.add, op1=ALU.max)
             return hid
 
-        def feed_forward(q, u, hid):
+        def feed_forward(pieces, u, hid):
             c, j = divmod(u, CHUNK)
-            nc.tensor.matmul(product[q], ff[c][:, j, :], hid, start=u == 0 and q != LAST, stop=u == U_BLOCKS - 1)
-            if u == U_BLOCKS - 1:
-                if q != LAST:
-                    added[q] = held.tile([P, WIDTHS[q]], F32, name=f"added{q}")[:]
-                    nc.vector.tensor_add(added[q], product[q], own[:, STARTS[q] : STARTS[q] + WIDTHS[q]])
-                for b in range(B):
-                    for i, (piece, lo, hi, first) in enumerate(parts[b]):
-                        if piece == q:
-                            nc.vector.bn_stats(stats[b][:, i, :], added[q][:, lo:hi])
-                            if i == len(parts[b]) - 1:
-                                normalise(b)
+            for q in pieces:
+                at = STARTS[q] - STARTS[pieces[0]]
+                nc.tensor.matmul(
+                    product[q],
+                    ff[c][:, j, :],
+                    hid[:, at : at + WIDTHS[q]],
+                    start=u == 0 and q != LAST,
+                    stop=u == U_BLOCKS - 1,
+                )
+                if u == U_BLOCKS - 1:
+                    finish(q)
+
+        def finish(q):
+            if q != LAST:
+                added[q] = held.tile([P, WIDTHS[q]], F32, name=f"added{q}")[:]
+                nc.vector.tensor_add(added[q], product[q], own[:, STARTS[q] : STARTS[q] + WIDTHS[q]])
+            for b in range(B):
+                for i, (piece, lo, hi, first) in enumerate(parts[b]):
+                    if piece == q:
+                        nc.vector.bn_stats(stats[b][:, i, :], added[q][:, lo:hi])
+                        if i == len(parts[b]) - 1:
+                            normalise(b)
 
         def normalise(b):
             mean_var = ring.tile([P, 2], F32, name="mean_var")
@@ -179,14 +199,14 @@ def tile_messagepassinglayer_b_kernel(
                     nc.sync.dma_start(out[:, first : first + hi - lo], normed[:])
 
         waiting = []
-        for q in range(PIECES):
-            if q == LAST:
-                nc.tensor.matmul(product[q], identity[:], own[:, STARTS[q] : STARTS[q] + WIDTHS[q]], start=True, stop=False)
-            for u in range(U_BLOCKS):
-                waiting.append((q, u, hidden_block(q, u)))
+        for pieces, from_block, to_block in SWEEPS:
+            if LAST in pieces and from_block == 0:
+                nc.tensor.matmul(product[LAST], identity[:], own[:, STARTS[LAST] :], start=True, stop=False)
+            for u in range(from_block, to_block):
+                waiting.append((pieces, u, hidden_block(pieces, u)))
                 if len(waiting) > LAG:
                     feed_forward(*waiting.pop(0))
-                if q == 0 and u + CHUNK < U_BLOCKS:
+                if pieces == SWEEPS[0][0] and u + CHUNK < U_BLOCKS:
                     round_step(u // CHUNK + 1, u % CHUNK)
         for late in waiting:
             feed_forward(*late)

import concourse.masks as masks
import concourse.mybir as mybir

BF16, F32, U16 = mybir.dt.bfloat16, mybir.dt.float32, mybir.dt.uint16
ACT = mybir.ActivationFunctionType
ALU = mybir.AluOpType

P = 128
B, S = 2, 768
M, U = 256, 4096
EPS = 1e-5
GROUPS = 3
GROUP = S // GROUPS
ROWS = GROUP // P
HALF = S // 2
M_BLOCKS = M // P
K_BLOCKS = 1 + M_BLOCKS
U_BLOCKS = U // P
CHUNK = 4
CHUNKS = U_BLOCKS // CHUNK
BANK = 512
WIDTHS = (BANK, BANK, BANK // 2, BANK // 2)
STARTS = tuple(sum(WIDTHS[:q]) for q in range(len(WIDTHS)))
PIECES = len(WIDTHS)
LAST = PIECES - 1
SPLIT = 2 * CHUNK
SWEEPS = (
    ((0,), 0, U_BLOCKS),
    ((1,), 0, U_BLOCKS),
    ((2, 3), 0, U_BLOCKS - SPLIT),
    ((2,), U_BLOCKS - SPLIT, U_BLOCKS),
    ((3,), U_BLOCKS - SPLIT, U_BLOCKS),
)
LAG = 8

FLOPS = 2 * B * S * (2 * P * M + (P + M) * U + U * P)


def tile_messagepassinglayer_b_kernel(
    tc, table, w_left, w_right, w_comb, b_comb, w_ff, norm_w, norm_b, offs, out
):
    nc = tc.nc
    with (
        tc.tile_pool(name="held", bufs=1) as held,
        tc.tile_pool(name="ring", bufs=2) as ring,
        tc.tile_pool(name="hids", bufs=LAG + 2) as hids,
        tc.psum_pool(name="sums", bufs=1) as sums,
        tc.psum_pool(name="work", bufs=4) as work,
    ):
        rows = [held.tile([P, GROUPS, ROWS, P], BF16, name=f"rows{b}") for b in range(B)]
        offsets = held.tile([P, B * 2 * S // 16], U16, name="offsets")
        left = held.tile([P, M], BF16, name="left")
        right = held.tile([P, M], BF16, name="right")
        bias = held.tile([P, CHUNKS, CHUNK], F32, name="bias")
        norm_w_column = held.tile([P, 1], F32, name="norm_w_column")
        norm_b_column = held.tile([P, 1], F32, name="norm_b_column")
        by_customer = table.rearrange("b (g p a) d -> b p g a d", g=GROUPS, a=ROWS)
        for g in range(GROUPS):
            nc.sync.dma_start(rows[0][:, g], by_customer[0][:, g])
        nc.sync.dma_start(rows[1][:], by_customer[1])
        nc.sync.dma_start(offsets[:], offs)
        nc.sync.dma_start(left[:], w_left)
        nc.sync.dma_start(right[:], w_right)
        comb_f32, ff_f32 = [], []
        for c in range(CHUNKS):
            span = slice(c * CHUNK * P, (c + 1) * CHUNK * P)
            comb_f32.append(held.tile([P, K_BLOCKS, CHUNK * P], F32, name=f"comb_f32_{c}"))
            nc.sync.dma_start(comb_f32[c][:], w_comb[:, span].rearrange("(k p) u -> p k u", p=P))
            ff_f32.append(held.tile([P, CHUNK, P], F32, name=f"ff_f32_{c}"))
            nc.sync.dma_start(ff_f32[c][:], w_ff[span, :].rearrange("(p j) c -> p j c", j=CHUNK))
            if c == 0:
                nc.sync.dma_start(bias[:], b_comb.rearrange("(c p j) o -> p c (j o)", p=P, j=CHUNK))
        nc.sync.dma_start(norm_w_column[:], norm_w)
        nc.sync.dma_start(norm_b_column[:], norm_b)

        identity = held.tile([P, P], BF16, name="identity")
        masks.make_identity(nc, identity[:])
        eps = held.tile([P, 1], F32, name="eps")
        nc.vector.memset(eps[:], EPS)
        warm = held.tile([P, 1], F32, name="warm")
        nc.scalar.activation(warm[:], eps[:], ACT.Abs_reciprocal_sqrt)

        window = [held.tile([P, S], BF16, name=f"window{b}") for b in range(B)]
        for b in range(B):
            for g in range(GROUPS):
                turned = work.tile([P, ROWS, P], BF16, tag="work", name="turned")
                for a in range(ROWS):
                    nc.tensor.transpose(turned[:, a, :], rows[b][:, g, a, :], identity[:])
                in_order = turned[:].rearrange("d a p -> d p a")
                columns_of = window[b][:, g * GROUP : (g + 1) * GROUP].rearrange("d (p a) -> d p a", a=ROWS)
                nc.scalar.copy(columns_of, in_order)

        own = held.tile([P, B * S], BF16, name="own")
        for b in range(B):
            nc.vector.tensor_copy(own[:, b * S : (b + 1) * S], window[b][:])

        comb = [held.tile([P, K_BLOCKS, CHUNK * P], BF16, name=f"comb{c}") for c in range(CHUNKS)]
        ff = [held.tile([P, CHUNK, P], BF16, name=f"ff{c}") for c in range(CHUNKS)]

        def round_step(c, step):
            if step < K_BLOCKS:
                nc.vector.tensor_copy(comb[c][:, step, :], comb_f32[c][:, step, :])
            else:
                nc.vector.tensor_copy(ff[c][:], ff_f32[c][:])

        for step in range(CHUNK):
            round_step(0, step)

        info = [held.tile([P, B * S], BF16, name=f"info{m}") for m in range(M_BLOCKS)]
        for b in range(B):
            for h in range(2):
                for m in range(M_BLOCKS):
                    both = work.tile([P, HALF], F32, tag="work", name="both")
                    for side, weights in enumerate((left, right)):
                        first = ((2 * b + side) * S + h * HALF) // 16
                        nc.tensor.matmul(
                            both[:],
                            weights[:, m * P : (m + 1) * P],
                            window[b][:].indirect(offsets[:, first : first + HALF // 16]),
                            start=side == 0,
                            stop=side == 1,
                        )
                    nc.scalar.copy(info[m][:, b * S + h * HALF : b * S + (h + 1) * HALF], both[:])

        banks = [sums.tile([P, BANK], F32, name=f"bank{q}") for q in range(PIECES)]
        product = [banks[q][:, : WIDTHS[q]] for q in range(PIECES)]
        added = {LAST: product[LAST]}
        moving = (own, info[0], info[1])
        parts = [[] for b in range(B)]
        for q in range(PIECES):
            for b in range(B):
                lo, hi = max(STARTS[q], b * S), min(STARTS[q] + WIDTHS[q], (b + 1) * S)
                if lo < hi:
                    parts[b].append((q, lo - STARTS[q], hi - STARTS[q], lo))
        stats = [held.tile([P, len(parts[b]), 6], F32, name=f"stats{b}") for b in range(B)]

        def hidden_block(pieces, u):
            c, j = divmod(u, CHUNK)
            begin, width = STARTS[pieces[0]], sum(WIDTHS[q] for q in pieces)
            pre = work.tile([P, width], F32, tag="work", name="pre")
            for k in range(K_BLOCKS):
                nc.tensor.matmul(
                    pre[:],
                    comb[c][:, k, :].rearrange("d (p j) -> d j p", j=CHUNK)[:, j, :],
                    moving[k][:, begin : begin + width],
                    start=k == 0,
                    stop=k == K_BLOCKS - 1,
                )
            hid = hids.tile([P, BANK], BF16, name="hid")[:, :width]
            if u % 2 == 0:
                nc.scalar.activation(hid, pre[:], ACT.Relu, bias=bias[:, c, j : j + 1])
            else:
                nc.vector.tensor_scalar(hid, pre[:], bias[:, c, j : j + 1], 0.0, op0=ALU.add, op1=ALU.max)
            return hid

        def feed_forward(pieces, u, hid):
            c, j = divmod(u, CHUNK)
            for q in pieces:
                at = STARTS[q] - STARTS[pieces[0]]
                nc.tensor.matmul(
                    product[q],
                    ff[c][:, j, :],
                    hid[:, at : at + WIDTHS[q]],
                    start=u == 0 and q != LAST,
                    stop=u == U_BLOCKS - 1,
                )
                if u == U_BLOCKS - 1:
                    finish(q)

        def finish(q):
            if q != LAST:
                added[q] = held.tile([P, WIDTHS[q]], F32, name=f"added{q}")[:]
                nc.vector.tensor_add(added[q], product[q], own[:, STARTS[q] : STARTS[q] + WIDTHS[q]])
            for b in range(B):
                for i, (piece, lo, hi, first) in enumerate(parts[b]):
                    if piece == q:
                        nc.vector.bn_stats(stats[b][:, i, :], added[q][:, lo:hi])
                        if i == len(parts[b]) - 1:
                            normalise(b)

        def normalise(b):
            mean_var = ring.tile([P, 2], F32, name="mean_var")
            nc.vector.bn_aggr(mean_var[:], stats[b][:].rearrange("p i s -> p (i s)"))
            inv_std = ring.tile([P, 1], F32, name="inv_std")
            nc.scalar.activation(inv_std[:], mean_var[:, 1:2], ACT.Abs_reciprocal_sqrt, bias=eps[:])
            minus_mean_w = ring.tile([P, 1], F32, name="minus_mean_w")
            nc.vector.tensor_scalar(minus_mean_w[:], mean_var[:, 0:1], norm_w_column[:], -1.0, op0=ALU.mult, op1=ALU.mult)
            gain = ring.tile([P, 1], F32, name="gain")
            nc.vector.tensor_mul(gain[:], inv_std[:], norm_w_column[:])
            shift = ring.tile([P, 1], F32, name="shift")
            nc.vector.tensor_scalar(shift[:], inv_std[:], minus_mean_w[:], norm_b_column[:], op0=ALU.mult, op1=ALU.add)
            for i, (q, lo, hi, first) in enumerate(parts[b]):
                normed = ring.tile([P, hi - lo], F32, name=f"normed{i}")
                if i % 2 == 0:
                    nc.vector.tensor_scalar(normed[:], added[q][:, lo:hi], gain[:], shift[:], op0=ALU.mult, op1=ALU.add)
                    nc.sync.dma_start(out[:, first : first + hi - lo], normed[:])
                else:
                    nc.scalar.activation(normed[:], added[q][:, lo:hi], ACT.Identity, bias=shift[:], scale=gain[:])
                    nc.sync.dma_start(out[:, first : first + hi - lo], normed[:])

        waiting = []
        for pieces, from_block, to_block in SWEEPS:
            if LAST in pieces and from_block == 0:
                nc.tensor.matmul(product[LAST], identity[:], own[:, STARTS[LAST] :], start=True, stop=False)
            for u in range(from_block, to_block):
                waiting.append((pieces, u, hidden_block(pieces, u)))
                if len(waiting) > LAG:
                    feed_forward(*waiting.pop(0))
                if pieces == SWEEPS[0][0] and u + CHUNK < U_BLOCKS:
                    round_step(u // CHUNK + 1, u % CHUNK)
        for late in waiting:
            feed_forward(*late)
